import numpy as np
import ml_dtypes


def mxq(x, axis, fmt="e4m3"):
    dtype, down = {"e4m3": (ml_dtypes.float8_e4m3fn, 7), "e5m2": (ml_dtypes.float8_e5m2, 14)}[fmt]
    v = np.moveaxis(np.asarray(x, np.float32).astype(ml_dtypes.bfloat16).astype(np.float64), axis, -1)
    blocks = v.reshape(v.shape[:-1] + (-1, 32))
    amax = np.abs(blocks).max(-1, keepdims=True)
    byte = np.maximum(np.where(amax > 0, np.frexp(amax)[1] - 1 + 127, 0) - down, 1)
    scale = np.exp2(byte - 127.0)
    codes = (blocks / scale).astype(np.float32).astype(dtype).astype(np.float64)
    return np.moveaxis((codes * scale).reshape(v.shape), -1, axis)


WIDE = False


def mx_kscale(k, group=512):
    if not WIDE:
        return np.ones(k)
    levels = np.array([10, -10, 5, -5, 0])
    if group != 512:
        return np.exp2(np.random.permutation(np.resize(levels, k // group))).repeat(group)
    if k % 512:
        return np.exp2(np.random.permutation(np.resize(levels, k // 32))).repeat(32)
    a = np.empty((k // 512, 16))
    for p in range(k // 512):
        a[p, :8] = np.random.permutation(np.resize(levels, 8))
        for g in range(8):
            far = levels[np.abs(levels - a[p, g]) >= 10]
            a[p, g + 8] = far[np.random.randint(len(far))]
    return np.exp2(a.ravel()).repeat(32)


BF16 = ml_dtypes.bfloat16


def bf(x):
    return np.asarray(x, np.float32).astype(BF16)


def f64(x):
    return np.asarray(x).astype(np.float64)


T, H, HD = 1024, 2, 512
W = H * HD


def sigmoid(v):
    return 1.0 / (1.0 + np.exp(-v))


def softplus(v):
    return np.log(1.0 + np.exp(v))


def heads(v):
    return v.reshape(T, H, HD).transpose(1, 0, 2)


def block_diag_linear(x, w, b):
    y = (heads(x) @ w).transpose(1, 0, 2) + b
    return y.reshape(T, W)


def setup_inputs():
    s = mx_kscale(T)
    s = (s / s.min())[:, None]
    u = mx_kscale(W, group=128)
    u = u / u.max()
    uh = u.reshape(H, 1, HD)
    x0 = bf(np.random.standard_normal((T, W)))
    state0 = bf(np.random.standard_normal((T, W)))
    w_in0 = bf(np.random.standard_normal((H, HD, HD)) / np.sqrt(HD))
    b_in = bf(np.random.standard_normal((H, HD)) * 0.5)
    w_a0 = bf(np.random.standard_normal((H, HD, HD)) / np.sqrt(HD))
    b_a = bf(np.random.standard_normal((H, HD)) * 0.5)
    a_param = bf(-2.0 + 0.5 * np.random.standard_normal(W))
    g = bf(np.random.standard_normal((T, W)) * np.exp2(np.random.randint(-6, 1, (T, 1))) * 4.0 / (s * s) * u)
    gate_x = sigmoid(block_diag_linear(f64(x0), f64(w_in0), f64(b_in)))
    gate_a = sigmoid(block_diag_linear(f64(x0), f64(w_a0), f64(b_a)))
    return {"x": bf(f64(x0) * s),
            "state": bf(f64(state0) * s),
            "w_in": bf(f64(w_in0) / uh),
            "b_in": b_in,
            "w_a": bf(f64(w_a0) / uh),
            "b_a": b_a,
            "a_param": a_param,
            "gate_x": np.asarray(gate_x, np.float32),
            "gate_a": np.asarray(gate_a, np.float32),
            "grad_out": g}


def reference(x, state, w_in, b_in, w_a, b_a, a_param, gate_x, gate_a, grad_out):
    xf = f64(x)
    g = f64(grad_out)
    gx = f64(gate_x)
    ga = f64(gate_a)
    log_a = -8.0 * ga * softplus(f64(a_param))
    a = np.exp(log_a)
    scale = np.sqrt(1.0 - np.exp(2.0 * log_a))
    dp_in = g * xf * scale * gx * (1.0 - gx)
    dp_a = g * (a * f64(state) - gx * xf * a * a / scale) * log_a * (1.0 - ga)
    dz = np.concatenate([heads(dp_in), heads(dp_a)], axis=2)
    w = np.concatenate([f64(w_in), f64(w_a)], axis=2)
    dxh = mxq(dz, 2, "e5m2") @ mxq(w, 2, "e4m3").transpose(0, 2, 1)
    dx = dxh.transpose(1, 0, 2).reshape(T, W) + g * gx * scale
    dw_a = mxq(heads(xf), 1, "e4m3").transpose(0, 2, 1) @ mxq(heads(dp_a), 1, "e5m2")
    return dx, dw_a

@@ -1,0 +1,529 @@
+from contextlib import ExitStack
+
+import concourse.mybir as mybir
+from concourse.masks import make_identity
+
+F32 = mybir.dt.float32
+BF16 = mybir.dt.bfloat16
+U32 = mybir.dt.uint32
+U8 = mybir.dt.uint8
+E4 = mybir.dt.float8_e4m3fn_x4
+E5 = mybir.dt.float8_e5m2_x4
+ACT = mybir.ActivationFunctionType
+ALU = mybir.AluOpType
+
+T, W, H, HD = 1024, 1024, 2, 512
+P = 128
+NG = 2
+NM = NG * H
+NC = 4 * NM
+
+FLOPS = 2 * T * HD * 2 * HD * H + 2 * HD * HD * T * H
+
+
+def tile_rglru_v_kernel(tc, x, state, w_in, b_in, w_a, b_a, a_param, gate_x, gate_a, grad_out, out_0, out_1):
+    nc = tc.nc
+
+    def tok(ap):
+        return ap.rearrange("(g p j) w -> g p j w", g=NG, j=4)
+
+    xv, sv, gv, gxv, gav, ov = tok(x), tok(state), tok(grad_out), tok(gate_x), tok(gate_a), tok(out_0)
+
+    with ExitStack() as ctx:
+        sb = ctx.enter_context(tc.tile_pool(name="sb", bufs=1))
+        ps = ctx.enter_context(tc.psum_pool(name="ps", bufs=1))
+        ctx.enter_context(tc.manual_schedule())
+
+        def st(shape, dt, tag, bufs):
+            return sb.tile(shape, dt, name=tag, tag=tag, bufs=bufs, align_bytes=64)
+
+        def bank(shape, tag, bufs):
+            return ps.tile(shape, F32, name=tag, tag=tag, bufs=bufs)
+
+        ap_t = st([P, H, 4], BF16, "apar", 1)
+        nc.sync.dma_start(out=ap_t[:], in_=a_param.rearrange("(h f t) -> f h t", h=H, t=4))
+        ident = st([P, P], F32, "ident", 1)
+        make_identity(nc, ident[:])
+        one = st([P, 1], F32, "one", 1)
+        negone = st([P, 1], F32, "negone", 1)
+        neghalf = st([P, 1], F32, "neghalf", 1)
+        nc.vector.memset(one[:], 1.0)
+        nc.vector.memset(negone[:], -1.0)
+        nc.vector.memset(neghalf[:], -0.5)
+
+        ga, gx, gt, stt, xt = {}, {}, {}, {}, {}
+
+        def load(dst, key, view, dt, tag, bufs, m):
+            g, h = m // H, m % H
+            t = st([P, 4, HD], dt, tag, bufs)
+            nc.sync.dma_start(out=t[:], in_=view[g, :, :, h * HD:(h + 1) * HD])
+            dst[key] = t
+
+        def load_ga(m):
+            load(ga, m, gav, F32, "ga", NM, m)
+
+        def load_gx(m):
+            load(gx, m, gxv, F32, "gx", 2, m)
+
+        def load_g(m):
+            load(gt, m, gv, BF16, "g", 2, m)
+
+        def load_s(m):
+            load(stt, m, sv, BF16, "s", 2, m)
+
+        def load_x(m):
+            load(xt, m, xv, BF16, "x", 2, m)
+
+        wraw = {}
+
+        def load_w(h):
+            t = st([P, 2, 4, HD], BF16, "e", 3)
+            nc.sync.dma_start(out=t[:, 0], in_=w_in[h].rearrange("(r p) o -> p r o", r=4))
+            nc.sync.dma_start(out=t[:, 1], in_=w_a[h].rearrange("(r p) o -> p r o", r=4))
+            wraw[h] = t
+
+        load_ga(0)
+        load_ga(1)
+        load_w(0)
+        load_g(0)
+        load_gx(0)
+        load_x(0)
+        load_s(0)
+        load_w(1)
+        load_ga(2)
+        load_ga(3)
+        load_g(1)
+        load_gx(1)
+        load_x(1)
+        load_s(1)
+
+        apf = ap_t[:].rearrange("p h t -> p (h t)")
+        nabs = st([P, 8], F32, "nabs", 1)
+        relu = st([P, 8], F32, "relu", 1)
+        u8 = st([P, 8], F32, "u8", 1)
+        l8 = st([P, 8], F32, "l8", 1)
+        sp = st([P, 8], F32, "sp", 1)
+        c8 = st([P, 8], F32, "c8", 1)
+        c16 = st([P, 8], F32, "c16", 1)
+        nc.vector.scalar_tensor_tensor(out=nabs[:], in0=apf, scalar=-1.0, in1=apf, op0=ALU.mult, op1=ALU.min)
+        nc.vector.tensor_scalar(out=relu[:], in0=apf, scalar1=0.0, scalar2=None, op0=ALU.max)
+        nc.scalar.activation(out=u8[:], in_=nabs[:], func=ACT.Exp)
+        nc.scalar.activation(out=l8[:], in_=u8[:], func=ACT.Ln, bias=one[:])
+        nc.vector.tensor_tensor(out=sp[:], in0=l8[:], in1=relu[:], op=ALU.add)
+        nc.vector.tensor_scalar(out=c16[:], in0=sp[:], scalar1=16.0, scalar2=None, op0=ALU.mult)
+        nc.vector.tensor_scalar(out=c8[:], in0=sp[:], scalar1=8.0, scalar2=None, op0=ALU.mult)
+
+        def mh(i):
+            return i // 4, (i // 4) % H, i % 4
+
+        gab, ea, qp, sc = {}, {}, {}, {}
+
+        def pe_ga(i):
+            m, h, t = mh(i)
+            b = bank([P, 4, P], "X", 4)
+            for j in range(4):
+                nc.tensor.transpose(b[:, j, :], ga[m][:, j, t::4], ident[:])
+            gab[i] = b
+
+        def s_e(i):
+            m, h, t = mh(i)
+            ea[i] = st([P, HD], F32, "EA", NC)
+            nc.scalar.activation(out=ea[i][:], in_=gab[i][:].rearrange("p j n -> p (j n)"), func=ACT.Exp,
+                                 scale=c16[:, 4 * h + t:4 * h + t + 1])
+
+        def s_q(i):
+            qp[i] = st([P, HD], F32, "qp", 4)
+            nc.scalar.activation(out=qp[i][:], in_=ea[i][:], func=ACT.Abs_reciprocal_sqrt, bias=negone[:])
+
+        def s_a(i):
+            nc.scalar.activation(out=ea[i][:], in_=ea[i][:], func=ACT.Abs_reciprocal_sqrt)
+
+        def s_p(i):
+            nc.scalar.activation(out=qp[i][:], in_=qp[i][:], func=ACT.Square)
+
+        def s_s(i):
+            sc[i] = st([P, 4, P], F32, "S", 2)
+            nc.scalar.activation(out=sc[i][:].rearrange("p j n -> p (j n)"), in_=qp[i][:],
+                                 func=ACT.Abs_reciprocal_sqrt, bias=one[:])
+
+        def s_sq(m):
+            v = ga[m][:].rearrange("p j w -> p (j w)")
+            nc.scalar.activation(out=v, in_=v, func=ACT.Square, bias=neghalf[:])
+
+        hh, tt = {}, {}
+
+        def g_h(i):
+            m, h, t = mh(i)
+            hh[i] = st([P, 4, P], F32, "h", 1)
+            nc.gpsimd.tensor_tensor(out=hh[i][:], in0=gt[m][:, :, t::4], in1=gx[m][:, :, t::4], op=ALU.mult)
+
+        def g_t(i):
+            m, h, t = mh(i)
+            tt[i] = st([P, 4, P], F32, "t", 2)
+            nc.gpsimd.tensor_tensor(out=tt[i][:], in0=gt[m][:, :, t::4], in1=stt[m][:, :, t::4], op=ALU.mult)
+
+        stb, tfb, ffb, dtb = {}, {}, {}, {}
+        ee, ff, dpa, nd = {}, {}, {}, {}
+        d1, d2 = {}, {}
+
+        def pe_st(i):
+            b = bank([P, 4, P], "ST", 1)
+            for j in range(4):
+                nc.tensor.transpose(b[:, j, :], sc[i][:, j, :], ident[:])
+            stb[i] = b
+
+        def v_e(i):
+            m, h, t = mh(i)
+            if t == 0:
+                ee[m] = st([P, 4, 4, P], F32, "e", 3)
+            nc.vector.tensor_tensor(out=ee[m][:, t], in0=stb[i][:], in1=hh[i][:], op=ALU.mult)
+
+        def v_f(i):
+            m, h, t = mh(i)
+            if t == 0:
+                ff[m] = st([P, 4, 4, P], F32, "f", 2)
+            nc.vector.scalar_tensor_tensor(out=ff[m][:, t], in0=ee[m][:, t], scalar=-1.0, in1=xt[m][:, :, t::4], op0=ALU.mult, op1=ALU.mult)
+
+        def pe_ff(i):
+            m, h, t = mh(i)
+            b = bank([P, 4, P], "FF", 1)
+            for j in range(4):
+                nc.tensor.transpose(b[:, j, :], ff[m][:, t, j, :], ident[:])
+            ffb[i] = b
+
+        def pe_tf(i):
+            b = bank([P, 4, P], "TF", 1)
+            for j in range(4):
+                nc.tensor.transpose(b[:, j, :], tt[i][:, j, :], ident[:])
+            tfb[i] = b
+
+        def v_d1(i):
+            m, h, t = mh(i)
+            d1[i] = st([P, 4, P], F32, "d1", 1)
+            nc.vector.scalar_tensor_tensor(out=d1[i][:].rearrange("p j n -> p (j n)"),
+                                           in0=tfb[i][:].rearrange("p j n -> p (j n)"),
+                                           scalar=c8[:, 4 * h + t:4 * h + t + 1],
+                                           in1=ea[i][:], op0=ALU.mult, op1=ALU.mult)
+
+        def v_d2(i):
+            m, h, t = mh(i)
+            d2[i] = st([P, 4, P], F32, "d2", 1)
+            nc.vector.scalar_tensor_tensor(out=d2[i][:].rearrange("p j n -> p (j n)"),
+                                           in0=ffb[i][:].rearrange("p j n -> p (j n)"),
+                                           scalar=c8[:, 4 * h + t:4 * h + t + 1],
+                                           in1=qp[i][:], op0=ALU.mult, op1=ALU.mult)
+
+        def pe_dt(i):
+            b = bank([P, 4, P], "DT", 1)
+            for j in range(4):
+                nc.tensor.matmul(b[:, j, :], lhsT=d1[i][:, j, :], rhs=ident[:], start=True, stop=False, is_transpose=True)
+                nc.tensor.matmul(b[:, j, :], lhsT=d2[i][:, j, :], rhs=ident[:], start=False, stop=True, is_transpose=True)
+            dtb[i] = b
+
+        def v_dpa(i):
+            m, h, t = mh(i)
+            if t == 0:
+                dpa[m] = st([P, 4, P, 4], BF16, "dpaT", 1)
+            nc.vector.scalar_tensor_tensor(out=dpa[m][:, t],
+                                           in0=ga[m][:, :, t::4].rearrange("p j f -> p f j"), scalar=0.25,
+                                           in1=dtb[i][:].rearrange("p j f -> p f j"),
+                                           op0=ALU.subtract, op1=ALU.mult)
+
+        def v_ndp(m, j):
+            if j == 0:
+                nd[m] = st([P, 4, HD], BF16, "ndp", 1)
+            nc.vector.scalar_tensor_tensor(out=nd[m][:, j, :].rearrange("p (f t) -> p f t", t=4),
+                                           in0=gx[m][:, j, :].rearrange("p (f t) -> p f t", t=4), scalar=1.0,
+                                           in1=ff[m][:, :, j, :].rearrange("p t f -> p f t"),
+                                           op0=ALU.subtract, op1=ALU.mult)
+
+        dib, dab, dif, daf = {}, {}, {}, {}
+        dinc, dafc, dtc = {}, {}, {}
+
+        def codes(tag, bufs):
+            return st([P, HD], U32, tag + "_c", bufs), st([P, HD], U8, tag + "_s", bufs)
+
+        def pe_di(m, q):
+            b = bank([P, 2, 2, P], "X", 4)
+            words = nd[m][:].bitcast(F32)
+            for r in range(2):
+                for u in range(2):
+                    nc.tensor.transpose(b[:, r, u, :], words[:, 2 * q + r, u::2], ident[:])
+            dib[m, q] = b
+
+        def s_di(m, q):
+            if q == 0:
+                dif[m] = st([P, 4, P, 4], BF16, "Fq", 2)
+            nc.scalar.copy(out=dif[m][:].bitcast(F32)[:, 2 * q:2 * q + 2], in_=dib[m, q][:].rearrange("p r u n -> p r n u"))
+
+        def pe_da(m, v):
+            b = bank([P, 4, P], "X", 4)
+            words = dpa[m][:].bitcast(F32)
+            for t in range(4):
+                nc.tensor.transpose(b[:, t, :], words[:, t, :, v], ident[:])
+            dab[m, v] = b
+
+        def s_da(m, v):
+            if v == 0:
+                daf[m] = st([P, 4, P, 4], BF16, "Fq", 2)
+            nc.scalar.copy(out=daf[m][:, 2 * v:2 * v + 2],
+                           in_=dab[m, v][:].bitcast(BF16).rearrange("p t (n e) -> p e n t", e=2))
+
+        def v_da(m, v):
+            if v == 0:
+                daf[m] = st([P, 4, P, 4], BF16, "Fq", 2)
+            nc.vector.tensor_copy(out=daf[m][:, 2 * v:2 * v + 2],
+                                  in_=dab[m, v][:].bitcast(BF16).rearrange("p t (n e) -> p e n t", e=2))
+
+        def v_quant(src, pair, fmt):
+            c, s = pair
+            nc.vector.quantize_mx(out=c[:].bitcast(fmt), scales=s[:], in_=src)
+
+        def v_qdi(m):
+            dinc[m] = codes("di", 1)
+            v_quant(dif[m][:].rearrange("p j n t -> p (j n t)"), dinc[m], E5)
+
+        def v_qda(m):
+            dafc[m] = codes("da", 1)
+            v_quant(daf[m][:].rearrange("p j n t -> p (j n t)"), dafc[m], E5)
+
+        def v_qdt(m):
+            dtc[m] = codes("dt", 4)
+            v_quant(dpa[m][:].rearrange("p t f j -> p (t f j)"), dtc[m], E5)
+
+        wb, wf, wc = {}, {}, {}
+
+        def pe_w(h, a, q):
+            b = bank([P, 2, 2, P], "X", 4)
+            words = wraw[h][:].bitcast(F32)
+            for r in range(2):
+                for u in range(2):
+                    nc.tensor.transpose(b[:, r, u, :], words[:, a, 2 * q + r, u::2], ident[:])
+            wb[h, a, q] = b
+
+        def v_w(h, a, q):
+            if q == 0:
+                wf[h, a] = st([P, 4, P, 4], BF16, "Fq", 2)
+            nc.vector.tensor_copy(out=wf[h, a][:].bitcast(F32)[:, 2 * q:2 * q + 2],
+                                  in_=wb[h, a, q][:].rearrange("p r u n -> p r n u"))
+
+        def v_qw(h, a):
+            wc[h, a] = codes("w", 4)
+            v_quant(wf[h, a][:].rearrange("p r n t -> p (r n t)"), wc[h, a], E4)
+
+        xi, xc = {}, {}
+
+        def v_xint(m, q):
+            xi[m, q] = st([P, 256, 4], BF16, "xi", 2)
+            nc.vector.tensor_copy(out=xi[m, q][:].rearrange("p (c i) t -> p c t i", i=4),
+                                  in_=xt[m][:, :, 256 * q:256 * (q + 1)].rearrange("p t (c i) -> p c t i", i=4))
+
+        def s_xint(m, q):
+            xi[m, q] = st([P, 256, 4], BF16, "xi", 2)
+            nc.scalar.copy(out=xi[m, q][:].rearrange("p (c i) t -> p c t i", i=4),
+                           in_=xt[m][:, :, 256 * q:256 * (q + 1)].rearrange("p t (c i) -> p c t i", i=4))
+
+        def v_qx(m, q):
+            if q == 0:
+                xc[m] = codes("x", 4)
+            c, s = xc[m]
+            nc.vector.quantize_mx(out=c[:, 256 * q:256 * (q + 1)].bitcast(E4), scales=s[:, 256 * q:256 * (q + 1)],
+                                  in_=xi[m, q][:].rearrange("p w j -> p (w j)"))
+
+        def v_qda_half(m, v):
+            if v == 0:
+                dafc[m] = codes("da", 1)
+            c, s = dafc[m]
+            cols = slice(256 * v, 256 * (v + 1))
+            nc.vector.quantize_mx(out=c[:, cols].bitcast(E5), scales=s[:, cols],
+                                  in_=daf[m][:, 2 * v:2 * v + 2].rearrange("p j n t -> p (j n t)"))
+
+        mmb, dwb = {}, {}
+
+        def pe_mm_part(m, j, n):
+            h = m % H
+            if n == 0:
+                mmb[m, j] = bank([P, HD], "X", 4)
+            cols = slice(j * P, (j + 1) * P)
+            d = (dinc, dafc)[n][m]
+            nc.tensor.matmul_mx(out=mmb[m, j][:], lhsT=d[0][:, cols].bitcast(E5), lhsT_scale=d[1][:, cols],
+                                rhs=wc[h, n][0][:].bitcast(E4), rhs_scale=wc[h, n][1][:],
+                                start=(n == 0), stop=(n == 1))
+
+        def pe_mm(m, j):
+            pe_mm_part(m, j, 0)
+            pe_mm_part(m, j, 1)
+
+        def v_fin(m, j):
+            g, h = m // H, m % H
+            o = st([P, HD], F32, "o", 4)
+            nc.vector.tensor_tensor(out=o[:].rearrange("p (f t) -> p f t", t=4),
+                                    in0=mmb[m, j][:].rearrange("p (f t) -> p f t", t=4),
+                                    in1=ee[m][:, :, j, :].rearrange("p t f -> p f t"), op=ALU.add)
+            nc.sync.dma_start(out=ov[g, :, j, h * HD:(h + 1) * HD], in_=o[:])
+
+        def pe_dw(h, c, tag="X", bufs=4):
+            b = bank([P, HD], tag, bufs)
+            cols = slice(c * P, (c + 1) * P)
+            for g in range(NG):
+                m = g * H + h
+                nc.tensor.matmul_mx(out=b[:], lhsT=xc[m][0][:, cols].bitcast(E4), lhsT_scale=xc[m][1][:, cols],
+                                    rhs=dtc[m][0][:].bitcast(E5), rhs_scale=dtc[m][1][:],
+                                    start=(g == 0), stop=(g == NG - 1))
+            dwb[h, c] = b
+
+        def s_dw(h, c, tag="o1", bufs=2):
+            o = st([P, HD], F32, tag, bufs)
+            nc.scalar.copy(out=o[:].rearrange("p (f t) -> p f t", t=4),
+                           in_=dwb[h, c][:].rearrange("p (t f) -> p f t", t=4))
+            nc.sync.dma_start(out=out_1[h, c * P:(c + 1) * P, :], in_=o[:])
+
+        plan = {}
+
+        def at(i, slot, fn, *args):
+            plan.setdefault((i, slot), []).append((fn, args))
+
+        def run(i, slot):
+            for fn, args in plan.get((i, slot), ()):
+                fn(*args)
+
+        def w_evac(h):
+            for a in (1, 0):
+                for q in range(2):
+                    pe_w(h, a, q)
+                    v_w(h, a, q)
+
+        def w_quant(h):
+            v_qw(h, 1)
+            v_qw(h, 0)
+
+        G1 = 8
+        at(0, "pe", w_evac, 1)
+        at(0, "end", w_quant, 1)
+        for k in range(G1, NC):
+            at(2, "end", pe_ga, k)
+            at(2, "end", s_e, k)
+        for m in range(NM):
+            for q in range(2):
+                if m == 0:
+                    at(2, "end", v_xint, m, q)
+                    at(2+1, "end", v_qx, m, q)
+                else:
+                    at(4 * m + 2, "x", s_xint, m, q)
+                    at(4 * m + 3, "end", v_qx, m, q)
+            if m:
+                at(4 * m, "s1", s_sq, m)
+        LAST = NM - 1
+        for m in range(NM):
+            b = 4 * m + 4
+            if m < LAST:
+                for j in range(2):
+                    at(b, "end", v_ndp, m, j)
+                at(b, "end", pe_di, m, 0)
+                at(b + 1, "s0", s_di, m, 0)
+                for v in range(2):
+                    at(b + 1, "pe", pe_da, m, v)
+                    at(b + 1, "pe", s_da, m, v)
+                for j in range(2, 4):
+                    at(b + 1, "end0", v_ndp, m, j)
+                at(b + 1, "end0", pe_di, m, 1)
+                at(b + 1, "end0", v_qdt, m)
+                at(b + 2, "s0", s_di, m, 1)
+                at(b + 2, "end", v_qda, m)
+                at(b + 2, "end", v_qdi, m)
+                for j in range(4):
+                    at(b + 2 + j, "end", pe_mm, m, j)
+                    at(b + 3 + j, "fin", v_fin, m, j)
+            else:
+                at(b, "p1", v_ndp, m, 0)
+                at(b, "p1", v_ndp, m, 1)
+                at(b, "p1", pe_di, m, 0)
+                at(b, "p1", s_di, m, 0)
+                at(b, "end", v_ndp, m, 2)
+                at(b, "end", v_ndp, m, 3)
+                at(b, "end", pe_di, m, 1)
+                at(b, "end", s_di, m, 1)
+                at(b + 1, "pe", pe_da, m, 0)
+                at(b + 1, "pe", s_da, m, 0)
+                at(b + 1, "pe", pe_da, m, 1)
+                at(b + 1, "pe", v_qdt, m)
+                at(b + 1, "pe", v_qdi, m)
+                at(b + 1, "pe", v_da, m, 1)
+                tags = ("ST", "FF", "TF", "DT")
+                at(b + 2, "fin", pe_mm_part, m, 0, 0)
+                at(b + 2, "fin", pe_mm_part, m, 1, 0)
+                for c in range(4):
+                    at(b + 2, "fin", pe_dw, 1, c, tags[c], 1)
+                at(b + 2, "fin", v_qda_half, m, 0)
+                at(b + 2, "fin", pe_mm_part, m, 0, 1)
+                at(b + 2, "fin", pe_mm_part, m, 1, 1)
+                at(b + 2, "fin", pe_mm_part, m, 2, 0)
+                at(b + 2, "fin", pe_mm_part, m, 3, 0)
+                at(b + 2, "fin", v_qda_half, m, 1)
+                at(b + 2, "fin", pe_mm_part, m, 2, 1)
+                at(b + 2, "fin", pe_mm_part, m, 3, 1)
+                for c in range(4):
+                    at(b + 2, "fin", s_dw, 1, c, ("S", "t")[c % 2], 2)
+                for j in range(4):
+                    at(b + 2, "fin2", v_fin, m, j)
+            if m == 2:
+                for c in range(4):
+                    at(b + 2 + c // 2, "end", pe_dw, 0, c)
+                    at(b + 3 + c // 2, "s0", s_dw, 0, c)
+            if m + 2 < NM:
+                at(b, "s0", load_g, m + 2)
+                at(b, "s0", load_s, m + 2)
+                at(b, "s0", load_x, m + 2)
+                at(b + 1, "end0", load_gx, m + 2)
+
+        for k in range(G1):
+            pe_ga(k)
+            s_e(k)
+        w_evac(0)
+        w_quant(0)
+        g_h(0)
+        g_t(0)
+        s_q(0)
+        s_q(1)
+        s_p(0)
+        s_a(0)
+        s_s(0)
+        pe_st(0)
+        s_p(1)
+        s_a(1)
+        s_s(1)
+        for i in range(NC + 8):
+            run(i, "s0")
+            if i + 2 < NC:
+                s_q(i + 2)
+                s_a(i + 2)
+                s_p(i + 2)
+                run(i, "s1")
+                s_s(i + 2)
+                if i == 0:
+                    s_sq(0)
+            run(i, "x")
+            if i < NC:
+                v_e(i)
+            if i + 1 < NC:
+                g_h(i + 1)
+                g_t(i + 1)
+                pe_st(i + 1)
+            if 1 <= i <= NC:
+                v_d1(i - 1)
+                v_d2(i - 1)
+            run(i, "p1")
+            if i < NC:
+                pe_tf(i)
+            if 2 <= i <= NC + 1:
+                v_dpa(i - 2)
+            if 1 <= i <= NC:
+                pe_dt(i - 1)
+            run(i, "fin")
+            run(i, "fin2")
+            run(i, "pe")
+            if i < NC:
+                v_f(i)
+                pe_ff(i)
+            run(i, "end0")
+            run(i, "end")

@@ -40,8 +40,10 @@ def tile_rglru_v_kernel(tc, x, state, w_in, b_in, w_a, b_a, a_param, gate_x, gat
         def bank(shape, tag, bufs):
             return ps.tile(shape, F32, name=tag, tag=tag, bufs=bufs)
 
-        ap_t = st([P, H, 4], BF16, "apar", 1)
-        nc.sync.dma_start(out=ap_t[:], in_=a_param.rearrange("(h f t) -> f h t", h=H, t=4))
+        rows = st([P, P], F32, "rows", 1)
+        nc.vector.memset(rows[:], 0.0)
+        raw = st([P, P], BF16, "apar", 1)
+        nc.sync.dma_start(out=raw[:8, :], in_=a_param.rearrange("(k p) -> k p", p=P))
         ident = st([P, P], F32, "ident", 1)
         make_identity(nc, ident[:])
         one = st([P, 1], F32, "one", 1)
@@ -97,7 +99,10 @@ def tile_rglru_v_kernel(tc, x, state, w_in, b_in, w_a, b_a, a_param, gate_x, gat
         load_x(1)
         load_s(1)
 
-        apf = ap_t[:].rearrange("p h t -> p (h t)")
+        nc.vector.tensor_copy(out=rows[:8, :], in_=raw[:8, :])
+        apb = bank([P, P], "ST", 1)
+        nc.tensor.transpose(apb[:], rows[:], ident[:])
+        apf = apb[:, 0:8]
         nabs = st([P, 8], F32, "nabs", 1)
         relu = st([P, 8], F32, "relu", 1)
         u8 = st([P, 8], F32, "u8", 1)
@@ -105,8 +110,8 @@ def tile_rglru_v_kernel(tc, x, state, w_in, b_in, w_a, b_a, a_param, gate_x, gat
         sp = st([P, 8], F32, "sp", 1)
         c8 = st([P, 8], F32, "c8", 1)
         c16 = st([P, 8], F32, "c16", 1)
-        nc.vector.scalar_tensor_tensor(out=nabs[:], in0=apf, scalar=-1.0, in1=apf, op0=ALU.mult, op1=ALU.min)
         nc.vector.tensor_scalar(out=relu[:], in0=apf, scalar1=0.0, scalar2=None, op0=ALU.max)
+        nc.vector.scalar_tensor_tensor(out=nabs[:], in0=relu[:], scalar=-2.0, in1=apf, op0=ALU.mult, op1=ALU.add)
         nc.scalar.activation(out=u8[:], in_=nabs[:], func=ACT.Exp)
         nc.scalar.activation(out=l8[:], in_=u8[:], func=ACT.Ln, bias=one[:])
         nc.vector.tensor_tensor(out=sp[:], in0=l8[:], in1=relu[:], op=ALU.add)
@@ -122,7 +127,7 @@ def tile_rglru_v_kernel(tc, x, state, w_in, b_in, w_a, b_a, a_param, gate_x, gat
             m, h, t = mh(i)
             b = bank([P, 4, P], "X", 4)
             for j in range(4):
-                nc.tensor.transpose(b[:, j, :], ga[m][:, j, t::4], ident[:])
+                nc.tensor.transpose(b[:, j, :], ga[m][:, j, t * P:(t + 1) * P], ident[:])
             gab[i] = b
 
         def s_e(i):
@@ -155,12 +160,12 @@ def tile_rglru_v_kernel(tc, x, state, w_in, b_in, w_a, b_a, a_param, gate_x, gat
         def g_h(i):
             m, h, t = mh(i)
             hh[i] = st([P, 4, P], F32, "h", 1)
-            nc.gpsimd.tensor_tensor(out=hh[i][:], in0=gt[m][:, :, t::4], in1=gx[m][:, :, t::4], op=ALU.mult)
+            nc.gpsimd.tensor_tensor(out=hh[i][:], in0=gt[m][:, :, t * P:(t + 1) * P], in1=gx[m][:, :, t * P:(t + 1) * P], op=ALU.mult)
 
         def g_t(i):
             m, h, t = mh(i)
             tt[i] = st([P, 4, P], F32, "t", 2)
-            nc.gpsimd.tensor_tensor(out=tt[i][:], in0=gt[m][:, :, t::4], in1=stt[m][:, :, t::4], op=ALU.mult)
+            nc.gpsimd.tensor_tensor(out=tt[i][:], in0=gt[m][:, :, t * P:(t + 1) * P], in1=stt[m][:, :, t * P:(t + 1) * P], op=ALU.mult)
 
         stb, tfb, ffb, dtb = {}, {}, {}, {}
         ee, ff, dpa, nd = {}, {}, {}, {}
@@ -175,20 +180,21 @@ def tile_rglru_v_kernel(tc, x, state, w_in, b_in, w_a, b_a, a_param, gate_x, gat
         def v_e(i):
             m, h, t = mh(i)
             if t == 0:
-                ee[m] = st([P, 4, 4, P], F32, "e", 3)
-            nc.vector.tensor_tensor(out=ee[m][:, t], in0=stb[i][:], in1=hh[i][:], op=ALU.mult)
+                ee[m] = st([P, 4, HD], F32, "e", 3)
+            nc.vector.tensor_tensor(out=ee[m][:, :, t * P:(t + 1) * P], in0=stb[i][:], in1=hh[i][:], op=ALU.mult)
 
         def v_f(i):
             m, h, t = mh(i)
             if t == 0:
-                ff[m] = st([P, 4, 4, P], F32, "f", 2)
-            nc.vector.scalar_tensor_tensor(out=ff[m][:, t], in0=ee[m][:, t], scalar=-1.0, in1=xt[m][:, :, t::4], op0=ALU.mult, op1=ALU.mult)
+                ff[m] = st([P, 4, HD], F32, "f", 2)
+            cols = slice(t * P, (t + 1) * P)
+            nc.vector.scalar_tensor_tensor(out=ff[m][:, :, cols], in0=ee[m][:, :, cols], scalar=-1.0, in1=xt[m][:, :, cols], op0=ALU.mult, op1=ALU.mult)
 
         def pe_ff(i):
             m, h, t = mh(i)
             b = bank([P, 4, P], "FF", 1)
             for j in range(4):
-                nc.tensor.transpose(b[:, j, :], ff[m][:, t, j, :], ident[:])
+                nc.tensor.transpose(b[:, j, :], ff[m][:, j, t * P:(t + 1) * P], ident[:])
             ffb[i] = b
 
         def pe_tf(i):
@@ -223,18 +229,16 @@ def tile_rglru_v_kernel(tc, x, state, w_in, b_in, w_a, b_a, a_param, gate_x, gat
         def v_dpa(i):
             m, h, t = mh(i)
             if t == 0:
-                dpa[m] = st([P, 4, P, 4], BF16, "dpaT", 1)
-            nc.vector.scalar_tensor_tensor(out=dpa[m][:, t],
-                                           in0=ga[m][:, :, t::4].rearrange("p j f -> p f j"), scalar=0.25,
+                dpa[m] = st([P, HD, 4], BF16, "dpaT", 1)
+            nc.vector.scalar_tensor_tensor(out=dpa[m][:, t * P:(t + 1) * P],
+                                           in0=ga[m][:, :, t * P:(t + 1) * P].rearrange("p j f -> p f j"), scalar=0.25,
                                            in1=dtb[i][:].rearrange("p j f -> p f j"),
                                            op0=ALU.subtract, op1=ALU.mult)
 
         def v_ndp(m, j):
             if j == 0:
                 nd[m] = st([P, 4, HD], BF16, "ndp", 1)
-            nc.vector.scalar_tensor_tensor(out=nd[m][:, j, :].rearrange("p (f t) -> p f t", t=4),
-                                           in0=gx[m][:, j, :].rearrange("p (f t) -> p f t", t=4), scalar=1.0,
-                                           in1=ff[m][:, :, j, :].rearrange("p t f -> p f t"),
+            nc.vector.scalar_tensor_tensor(out=nd[m][:, j, :], in0=gx[m][:, j, :], scalar=1.0, in1=ff[m][:, j, :],
                                            op0=ALU.subtract, op1=ALU.mult)
 
         dib, dab, dif, daf = {}, {}, {}, {}
@@ -260,7 +264,7 @@ def tile_rglru_v_kernel(tc, x, state, w_in, b_in, w_a, b_a, a_param, gate_x, gat
             b = bank([P, 4, P], "X", 4)
             words = dpa[m][:].bitcast(F32)
             for t in range(4):
-                nc.tensor.transpose(b[:, t, :], words[:, t, :, v], ident[:])
+                nc.tensor.transpose(b[:, t, :], words[:, t::4, v], ident[:])
             dab[m, v] = b
 
         def s_da(m, v):
@@ -289,7 +293,7 @@ def tile_rglru_v_kernel(tc, x, state, w_in, b_in, w_a, b_a, a_param, gate_x, gat
 
         def v_qdt(m):
             dtc[m] = codes("dt", 4)
-            v_quant(dpa[m][:].rearrange("p t f j -> p (t f j)"), dtc[m], E5)
+            v_quant(dpa[m][:].rearrange("p w j -> p (w j)"), dtc[m], E5)
 
         wb, wf, wc = {}, {}, {}
 
@@ -357,9 +361,7 @@ def tile_rglru_v_kernel(tc, x, state, w_in, b_in, w_a, b_a, a_param, gate_x, gat
         def v_fin(m, j):
             g, h = m // H, m % H
             o = st([P, HD], F32, "o", 4)
-            nc.vector.tensor_tensor(out=o[:].rearrange("p (f t) -> p f t", t=4),
-                                    in0=mmb[m, j][:].rearrange("p (f t) -> p f t", t=4),
-                                    in1=ee[m][:, :, j, :].rearrange("p t f -> p f t"), op=ALU.add)
+            nc.vector.tensor_tensor(out=o[:], in0=mmb[m, j][:], in1=ee[m][:, j, :], op=ALU.add)
             nc.sync.dma_start(out=ov[g, :, j, h * HD:(h + 1) * HD], in_=o[:])
 
         def pe_dw(h, c, tag="X", bufs=4):
@@ -374,8 +376,7 @@ def tile_rglru_v_kernel(tc, x, state, w_in, b_in, w_a, b_a, a_param, gate_x, gat
 
         def s_dw(h, c, tag="o1", bufs=2):
             o = st([P, HD], F32, tag, bufs)
-            nc.scalar.copy(out=o[:].rearrange("p (f t) -> p f t", t=4),
-                           in_=dwb[h, c][:].rearrange("p (t f) -> p f t", t=4))
+            nc.scalar.copy(out=o[:], in_=dwb[h, c][:])
             nc.sync.dma_start(out=out_1[h, c * P:(c + 1) * P, :], in_=o[:])
 
         plan = {}

@@ -18,6 +18,11 @@ NG = 2
 NM = NG * H
 NC = 4 * NM
 
+VADD = 0
+FLAST = False
+HB = 2
+HEADWARM = 0
+NW = lambda k, i: 3 if k == "ST" and i else 0
 FLOPS = 2 * T * HD * 2 * HD * H + 2 * HD * HD * T * H
 
 
@@ -52,6 +57,9 @@ def tile_rglru_v_kernel(tc, x, state, w_in, b_in, w_a, b_a, a_param, gate_x, gat
         nc.vector.memset(one[:], 1.0)
         nc.vector.memset(negone[:], -1.0)
         nc.vector.memset(neghalf[:], -0.5)
+
+        def pe_warm(b):
+            nc.tensor.matmul(b[:, 0, :], lhsT=ident[:], rhs=ident[:], start=True, stop=True)
 
         ga, gx, gt, stt, xt = {}, {}, {}, {}, {}
 
@@ -100,6 +108,8 @@ def tile_rglru_v_kernel(tc, x, state, w_in, b_in, w_a, b_a, a_param, gate_x, gat
         load_s(1)
 
         nc.vector.tensor_copy(out=rows[:8, :], in_=raw[:8, :])
+        for n in range(HEADWARM):
+            pe_warm(bank([P, 4, P], "DT", 1))
         apb = bank([P, P], "ST", 1)
         nc.tensor.transpose(apb[:], rows[:], ident[:])
         apf = apb[:, 0:8]
@@ -126,6 +136,8 @@ def tile_rglru_v_kernel(tc, x, state, w_in, b_in, w_a, b_a, a_param, gate_x, gat
         def pe_ga(i):
             m, h, t = mh(i)
             b = bank([P, 4, P], "X", 4)
+            for rep in range(NW("GA", i)):
+                pe_warm(b)
             for j in range(4):
                 nc.tensor.transpose(b[:, j, :], ga[m][:, j, t * P:(t + 1) * P], ident[:])
             gab[i] = b
@@ -159,8 +171,10 @@ def tile_rglru_v_kernel(tc, x, state, w_in, b_in, w_a, b_a, a_param, gate_x, gat
 
         def g_h(i):
             m, h, t = mh(i)
-            hh[i] = st([P, 4, P], F32, "h", 1)
-            nc.gpsimd.tensor_tensor(out=hh[i][:], in0=gt[m][:, :, t * P:(t + 1) * P], in1=gx[m][:, :, t * P:(t + 1) * P], op=ALU.mult)
+            hh[i] = st([P, 5, P], F32, "h", HB)
+            if HB == 2:
+                nc.gpsimd.memset(hh[i][:, 4, 0:1], -1.0)
+            nc.gpsimd.tensor_tensor(out=hh[i][:, 0:4], in0=gt[m][:, :, t * P:(t + 1) * P], in1=gx[m][:, :, t * P:(t + 1) * P], op=ALU.mult)
 
         def g_t(i):
             m, h, t = mh(i)
@@ -173,6 +187,8 @@ def tile_rglru_v_kernel(tc, x, state, w_in, b_in, w_a, b_a, a_param, gate_x, gat
 
         def pe_st(i):
             b = bank([P, 4, P], "ST", 1)
+            for rep in range(NW("ST", i)):
+                pe_warm(b)
             for j in range(4):
                 nc.tensor.transpose(b[:, j, :], sc[i][:, j, :], ident[:])
             stb[i] = b
@@ -181,24 +197,28 @@ def tile_rglru_v_kernel(tc, x, state, w_in, b_in, w_a, b_a, a_param, gate_x, gat
             m, h, t = mh(i)
             if t == 0:
                 ee[m] = st([P, 4, HD], F32, "e", 3)
-            nc.vector.tensor_tensor(out=ee[m][:, :, t * P:(t + 1) * P], in0=stb[i][:], in1=hh[i][:], op=ALU.mult)
+            nc.vector.tensor_tensor(out=ee[m][:, :, t * P:(t + 1) * P], in0=stb[i][:], in1=hh[i][:, 0:4], op=ALU.mult)
 
         def v_f(i):
             m, h, t = mh(i)
             if t == 0:
                 ff[m] = st([P, 4, HD], F32, "f", 2)
             cols = slice(t * P, (t + 1) * P)
-            nc.vector.scalar_tensor_tensor(out=ff[m][:, :, cols], in0=ee[m][:, :, cols], scalar=-1.0, in1=xt[m][:, :, cols], op0=ALU.mult, op1=ALU.mult)
+            nc.vector.scalar_tensor_tensor(out=ff[m][:, :, cols], in0=ee[m][:, :, cols], scalar=hh[i][:, 4, 0:1] if HB == 2 else -1.0, in1=xt[m][:, :, cols], op0=ALU.mult, op1=ALU.mult)
 
         def pe_ff(i):
             m, h, t = mh(i)
             b = bank([P, 4, P], "FF", 1)
+            for rep in range(NW("FF", i)):
+                pe_warm(b)
             for j in range(4):
                 nc.tensor.transpose(b[:, j, :], ff[m][:, j, t * P:(t + 1) * P], ident[:])
             ffb[i] = b
 
         def pe_tf(i):
             b = bank([P, 4, P], "TF", 1)
+            for rep in range(NW("TF", i)):
+                pe_warm(b)
             for j in range(4):
                 nc.tensor.transpose(b[:, j, :], tt[i][:, j, :], ident[:])
             tfb[i] = b
@@ -219,9 +239,15 @@ def tile_rglru_v_kernel(tc, x, state, w_in, b_in, w_a, b_a, a_param, gate_x, gat
                                            scalar=c8[:, 4 * h + t:4 * h + t + 1],
                                            in1=qp[i][:], op0=ALU.mult, op1=ALU.mult)
 
+        def v_add(i):
+            nc.vector.tensor_tensor(out=d1[i][:], in0=d1[i][:], in1=d2[i][:], op=ALU.add)
+
         def pe_dt(i):
             b = bank([P, 4, P], "DT", 1)
             for j in range(4):
+                if i < VADD:
+                    nc.tensor.transpose(b[:, j, :], d1[i][:, j, :], ident[:])
+                    continue
                 nc.tensor.matmul(b[:, j, :], lhsT=d1[i][:, j, :], rhs=ident[:], start=True, stop=False, is_transpose=True)
                 nc.tensor.matmul(b[:, j, :], lhsT=d2[i][:, j, :], rhs=ident[:], start=False, stop=True, is_transpose=True)
             dtb[i] = b
@@ -299,6 +325,8 @@ def tile_rglru_v_kernel(tc, x, state, w_in, b_in, w_a, b_a, a_param, gate_x, gat
 
         def pe_w(h, a, q):
             b = bank([P, 2, 2, P], "X", 4)
+            if NW("W", 4 * h + 2 * (1 - a) + q):
+                pe_warm(b[:, 0])
             words = wraw[h][:].bitcast(F32)
             for r in range(2):
                 for u in range(2):
@@ -380,6 +408,7 @@ def tile_rglru_v_kernel(tc, x, state, w_in, b_in, w_a, b_a, a_param, gate_x, gat
             nc.sync.dma_start(out=out_1[h, c * P:(c + 1) * P, :], in_=o[:])
 
         plan = {}
+        ADDS = []
 
         def at(i, slot, fn, *args):
             plan.setdefault((i, slot), []).append((fn, args))
@@ -484,6 +513,9 @@ def tile_rglru_v_kernel(tc, x, state, w_in, b_in, w_a, b_a, a_param, gate_x, gat
         w_quant(0)
         g_h(0)
         g_t(0)
+        if HB == 2:
+            g_h(1)
+            g_t(1)
         s_q(0)
         s_q(1)
         s_p(0)
@@ -507,24 +539,38 @@ def tile_rglru_v_kernel(tc, x, state, w_in, b_in, w_a, b_a, a_param, gate_x, gat
             if i < NC:
                 v_e(i)
             if i + 1 < NC:
-                g_h(i + 1)
-                g_t(i + 1)
+                if HB == 1:
+                    g_h(i + 1)
+                    g_t(i + 1)
                 pe_st(i + 1)
             if 1 <= i <= NC:
                 v_d1(i - 1)
                 v_d2(i - 1)
+                if i - 1 < VADD:
+                    ADDS.append(i - 1)
             run(i, "p1")
             if i < NC:
                 pe_tf(i)
             if 2 <= i <= NC + 1:
                 v_dpa(i - 2)
+            if ADDS:
+                v_add(ADDS.pop())
             if 1 <= i <= NC:
                 pe_dt(i - 1)
             run(i, "fin")
             run(i, "fin2")
+            while ADDS:
+                v_add(ADDS.pop())
             run(i, "pe")
             if i < NC:
-                v_f(i)
-                pe_ff(i)
+                if not FLAST:
+                    v_f(i)
+                    pe_ff(i)
             run(i, "end0")
             run(i, "end")
+            if i < NC and FLAST:
+                v_f(i)
+                pe_ff(i)
+            if HB == 2 and i + 2 < NC:
+                g_h(i + 2)
+                g_t(i + 2)

@@ -18,11 +18,20 @@ NG = 2
 NM = NG * H
 NC = 4 * NM
 
+ORDER = "A0 A1 W0 G0 Y0 X0 S0 A2 W1 A3 G1 Y1 X1 S1"
+W0AT = -1
+W1AT = 0
+W1SL = "p1"
+EIT = 0
+EITSL = "p1"
+X0AT = 0
+OB = 4
 VADD = 0
+VX = ()
 FLAST = False
 HB = 2
 HEADWARM = 0
-NW = lambda k, i: 3 if k == "ST" and i else 0
+NW = lambda k, i: 2 if k == "ST" else 0
 FLOPS = 2 * T * HD * 2 * HD * H + 2 * HD * HD * T * H
 
 
@@ -70,7 +79,7 @@ def tile_rglru_v_kernel(tc, x, state, w_in, b_in, w_a, b_a, a_param, gate_x, gat
             dst[key] = t
 
         def load_ga(m):
-            load(ga, m, gav, F32, "ga", NM, m)
+            load(ga, m, gav, F32, "ga", NM + 1, m)
 
         def load_gx(m):
             load(gx, m, gxv, F32, "gx", 2, m)
@@ -92,20 +101,9 @@ def tile_rglru_v_kernel(tc, x, state, w_in, b_in, w_a, b_a, a_param, gate_x, gat
             nc.sync.dma_start(out=t[:, 1], in_=w_a[h].rearrange("(r p) o -> p r o", r=4))
             wraw[h] = t
 
-        load_ga(0)
-        load_ga(1)
-        load_w(0)
-        load_g(0)
-        load_gx(0)
-        load_x(0)
-        load_s(0)
-        load_w(1)
-        load_ga(2)
-        load_ga(3)
-        load_g(1)
-        load_gx(1)
-        load_x(1)
-        load_s(1)
+        LOADS = dict(A=load_ga, G=load_g, Y=load_gx, X=load_x, S=load_s, W=load_w)
+        for key in ORDER.split():
+            LOADS[key[0]](int(key[1]))
 
         nc.vector.tensor_copy(out=rows[:8, :], in_=raw[:8, :])
         for n in range(HEADWARM):
@@ -163,18 +161,20 @@ def tile_rglru_v_kernel(tc, x, state, w_in, b_in, w_a, b_a, a_param, gate_x, gat
             nc.scalar.activation(out=sc[i][:].rearrange("p j n -> p (j n)"), in_=qp[i][:],
                                  func=ACT.Abs_reciprocal_sqrt, bias=one[:])
 
+        sq = {}
+
         def s_sq(m):
-            v = ga[m][:].rearrange("p j w -> p (j w)")
-            nc.scalar.activation(out=v, in_=v, func=ACT.Square, bias=neghalf[:])
+            sq[m] = st([P, HD, 4], F32, "ga", NM + 1)
+            nc.scalar.activation(out=sq[m][:], in_=ga[m][:].rearrange("p j w -> p w j"), func=ACT.Square, bias=neghalf[:])
 
         hh, tt = {}, {}
 
         def g_h(i):
             m, h, t = mh(i)
-            hh[i] = st([P, 5, P], F32, "h", HB)
+            hh[i] = st([P, 4 * P + 8], F32, "h", HB)
             if HB == 2:
-                nc.gpsimd.memset(hh[i][:, 4, 0:1], -1.0)
-            nc.gpsimd.tensor_tensor(out=hh[i][:, 0:4], in0=gt[m][:, :, t * P:(t + 1) * P], in1=gx[m][:, :, t * P:(t + 1) * P], op=ALU.mult)
+                nc.gpsimd.memset(hh[i][:, 4 * P:4 * P + 1], -1.0)
+            nc.gpsimd.tensor_tensor(out=hh[i][:, :4 * P].rearrange("p (j f) -> p j f", j=4), in0=gt[m][:, :, t * P:(t + 1) * P], in1=gx[m][:, :, t * P:(t + 1) * P], op=ALU.mult)
 
         def g_t(i):
             m, h, t = mh(i)
@@ -197,14 +197,14 @@ def tile_rglru_v_kernel(tc, x, state, w_in, b_in, w_a, b_a, a_param, gate_x, gat
             m, h, t = mh(i)
             if t == 0:
                 ee[m] = st([P, 4, HD], F32, "e", 3)
-            nc.vector.tensor_tensor(out=ee[m][:, :, t * P:(t + 1) * P], in0=stb[i][:], in1=hh[i][:, 0:4], op=ALU.mult)
+            nc.vector.tensor_tensor(out=ee[m][:, :, t * P:(t + 1) * P], in0=stb[i][:], in1=hh[i][:, :4 * P].rearrange("p (j f) -> p j f", j=4), op=ALU.mult)
 
         def v_f(i):
             m, h, t = mh(i)
             if t == 0:
                 ff[m] = st([P, 4, HD], F32, "f", 2)
             cols = slice(t * P, (t + 1) * P)
-            nc.vector.scalar_tensor_tensor(out=ff[m][:, :, cols], in0=ee[m][:, :, cols], scalar=hh[i][:, 4, 0:1] if HB == 2 else -1.0, in1=xt[m][:, :, cols], op0=ALU.mult, op1=ALU.mult)
+            nc.vector.scalar_tensor_tensor(out=ff[m][:, :, cols], in0=ee[m][:, :, cols], scalar=hh[i][:, 4 * P:4 * P + 1] if HB == 2 else -1.0, in1=xt[m][:, :, cols], op0=ALU.mult, op1=ALU.mult)
 
         def pe_ff(i):
             m, h, t = mh(i)
@@ -257,14 +257,15 @@ def tile_rglru_v_kernel(tc, x, state, w_in, b_in, w_a, b_a, a_param, gate_x, gat
             if t == 0:
                 dpa[m] = st([P, HD, 4], BF16, "dpaT", 1)
             nc.vector.scalar_tensor_tensor(out=dpa[m][:, t * P:(t + 1) * P],
-                                           in0=ga[m][:, :, t * P:(t + 1) * P].rearrange("p j f -> p f j"), scalar=0.25,
+                                           in0=sq[m][:, t * P:(t + 1) * P], scalar=0.25,
                                            in1=dtb[i][:].rearrange("p j f -> p f j"),
                                            op0=ALU.subtract, op1=ALU.mult)
 
-        def v_ndp(m, j):
-            if j == 0:
+        def v_ndp(m, q):
+            if q == 0:
                 nd[m] = st([P, 4, HD], BF16, "ndp", 1)
-            nc.vector.scalar_tensor_tensor(out=nd[m][:, j, :], in0=gx[m][:, j, :], scalar=1.0, in1=ff[m][:, j, :],
+            js = slice(2 * q, 2 * q + 2)
+            nc.vector.scalar_tensor_tensor(out=nd[m][:, js], in0=gx[m][:, js], scalar=1.0, in1=ff[m][:, js],
                                            op0=ALU.subtract, op1=ALU.mult)
 
         dib, dab, dif, daf = {}, {}, {}, {}
@@ -345,22 +346,19 @@ def tile_rglru_v_kernel(tc, x, state, w_in, b_in, w_a, b_a, a_param, gate_x, gat
 
         xi, xc = {}, {}
 
-        def v_xint(m, q):
-            xi[m, q] = st([P, 256, 4], BF16, "xi", 2)
-            nc.vector.tensor_copy(out=xi[m, q][:].rearrange("p (c i) t -> p c t i", i=4),
-                                  in_=xt[m][:, :, 256 * q:256 * (q + 1)].rearrange("p t (c i) -> p c t i", i=4))
+        def x_int(m, copy):
+            xi[m] = st([P, HD, 4], BF16, "ndp", 1)
+            copy(out=xi[m][:].rearrange("p (c i) t -> p c t i", i=4), in_=xt[m][:].rearrange("p t (c i) -> p c t i", i=4))
 
-        def s_xint(m, q):
-            xi[m, q] = st([P, 256, 4], BF16, "xi", 2)
-            nc.scalar.copy(out=xi[m, q][:].rearrange("p (c i) t -> p c t i", i=4),
-                           in_=xt[m][:, :, 256 * q:256 * (q + 1)].rearrange("p t (c i) -> p c t i", i=4))
+        def v_xint(m):
+            x_int(m, nc.vector.tensor_copy)
 
-        def v_qx(m, q):
-            if q == 0:
-                xc[m] = codes("x", 4)
-            c, s = xc[m]
-            nc.vector.quantize_mx(out=c[:, 256 * q:256 * (q + 1)].bitcast(E4), scales=s[:, 256 * q:256 * (q + 1)],
-                                  in_=xi[m, q][:].rearrange("p w j -> p (w j)"))
+        def s_xint(m):
+            x_int(m, nc.scalar.copy)
+
+        def v_qx(m):
+            xc[m] = codes("x", 4)
+            v_quant(xi[m][:].rearrange("p w j -> p (w j)"), xc[m], E4)
 
         def v_qda_half(m, v):
             if v == 0:
@@ -388,7 +386,7 @@ def tile_rglru_v_kernel(tc, x, state, w_in, b_in, w_a, b_a, a_param, gate_x, gat
 
         def v_fin(m, j):
             g, h = m // H, m % H
-            o = st([P, HD], F32, "o", 4)
+            o = st([P, HD], F32, "o", OB)
             nc.vector.tensor_tensor(out=o[:], in0=mmb[m, j][:], in1=ee[m][:, j, :], op=ALU.add)
             nc.sync.dma_start(out=ov[g, :, j, h * HD:(h + 1) * HD], in_=o[:])
 
@@ -402,7 +400,7 @@ def tile_rglru_v_kernel(tc, x, state, w_in, b_in, w_a, b_a, a_param, gate_x, gat
                                     start=(g == 0), stop=(g == NG - 1))
             dwb[h, c] = b
 
-        def s_dw(h, c, tag="o1", bufs=2):
+        def s_dw(h, c, tag, bufs):
             o = st([P, HD], F32, tag, bufs)
             nc.scalar.copy(out=o[:], in_=dwb[h, c][:])
             nc.sync.dma_start(out=out_1[h, c * P:(c + 1) * P, :], in_=o[:])
@@ -428,34 +426,37 @@ def tile_rglru_v_kernel(tc, x, state, w_in, b_in, w_a, b_a, a_param, gate_x, gat
             v_qw(h, 0)
 
         G1 = 8
-        at(0, "pe", w_evac, 1)
-        at(0, "end", w_quant, 1)
+        if W0AT >= 0:
+            at(W0AT, "pe", w_evac, 0)
+            at(W0AT, "end", w_quant, 0)
+        at(W1AT, W1SL, w_evac, 1)
+        at(W1AT, "end", w_quant, 1)
         for k in range(G1, NC):
-            at(2, "end", pe_ga, k)
-            at(2, "end", s_e, k)
+            at(EIT, EITSL, pe_ga, k)
+            at(EIT, EITSL, s_e, k)
         for m in range(NM):
-            for q in range(2):
-                if m == 0:
-                    at(2, "end", v_xint, m, q)
-                    at(2+1, "end", v_qx, m, q)
+            if m == 0:
+                at(X0AT, "end", v_xint, m)
+                at(X0AT + 1, "end", v_qx, m)
+            else:
+                if m in VX:
+                    at(4 * m + 2, "end", v_xint, m)
                 else:
-                    at(4 * m + 2, "x", s_xint, m, q)
-                    at(4 * m + 3, "end", v_qx, m, q)
+                    at(4 * m + 2, "x", s_xint, m)
+                at(4 * m + 3, "end", v_qx, m)
             if m:
                 at(4 * m, "s1", s_sq, m)
         LAST = NM - 1
         for m in range(NM):
             b = 4 * m + 4
             if m < LAST:
-                for j in range(2):
-                    at(b, "end", v_ndp, m, j)
+                at(b, "end", v_ndp, m, 0)
                 at(b, "end", pe_di, m, 0)
                 at(b + 1, "s0", s_di, m, 0)
                 for v in range(2):
                     at(b + 1, "pe", pe_da, m, v)
                     at(b + 1, "pe", s_da, m, v)
-                for j in range(2, 4):
-                    at(b + 1, "end0", v_ndp, m, j)
+                at(b + 1, "end0", v_ndp, m, 1)
                 at(b + 1, "end0", pe_di, m, 1)
                 at(b + 1, "end0", v_qdt, m)
                 at(b + 2, "s0", s_di, m, 1)
@@ -466,11 +467,9 @@ def tile_rglru_v_kernel(tc, x, state, w_in, b_in, w_a, b_a, a_param, gate_x, gat
                     at(b + 3 + j, "fin", v_fin, m, j)
             else:
                 at(b, "p1", v_ndp, m, 0)
-                at(b, "p1", v_ndp, m, 1)
                 at(b, "p1", pe_di, m, 0)
                 at(b, "p1", s_di, m, 0)
-                at(b, "end", v_ndp, m, 2)
-                at(b, "end", v_ndp, m, 3)
+                at(b, "end", v_ndp, m, 1)
                 at(b, "end", pe_di, m, 1)
                 at(b, "end", s_di, m, 1)
                 at(b + 1, "pe", pe_da, m, 0)
@@ -499,7 +498,7 @@ def tile_rglru_v_kernel(tc, x, state, w_in, b_in, w_a, b_a, a_param, gate_x, gat
             if m == 2:
                 for c in range(4):
                     at(b + 2 + c // 2, "end", pe_dw, 0, c)
-                    at(b + 3 + c // 2, "s0", s_dw, 0, c)
+                    at(b + 3 + c // 2, "s0", s_dw, 0, c, "o", OB)
             if m + 2 < NM:
                 at(b, "s0", load_g, m + 2)
                 at(b, "s0", load_s, m + 2)
@@ -509,8 +508,9 @@ def tile_rglru_v_kernel(tc, x, state, w_in, b_in, w_a, b_a, a_param, gate_x, gat
         for k in range(G1):
             pe_ga(k)
             s_e(k)
-        w_evac(0)
-        w_quant(0)
+        if W0AT < 0:
+            w_evac(0)
+            w_quant(0)
         g_h(0)
         g_t(0)
         if HB == 2:

@@ -18,7 +18,7 @@ NG = 2
 NM = NG * H
 NC = 4 * NM
 
-ORDER = "A0 A1 W0 G0 Y0 X0 S0 A2 W1 A3 G1 Y1 X1 S1"
+ORDER = "A0 A1 W0 G0 Y0 X0 S0 W1 A2 A3 G1 Y1 X1 S1"
 W0AT = -1
 W1AT = 0
 W1SL = "p1"
@@ -31,7 +31,7 @@ VX = ()
 FLAST = False
 HB = 2
 HEADWARM = 0
-NW = lambda k, i: 2 if k == "ST" else 0
+NW = lambda k, i: 3 if k == "ST" else 0
 FLOPS = 2 * T * HD * 2 * HD * H + 2 * HD * HD * T * H
 
 
@@ -97,8 +97,8 @@ def tile_rglru_v_kernel(tc, x, state, w_in, b_in, w_a, b_a, a_param, gate_x, gat
 
         def load_w(h):
             t = st([P, 2, 4, HD], BF16, "e", 3)
-            nc.sync.dma_start(out=t[:, 0], in_=w_in[h].rearrange("(r p) o -> p r o", r=4))
-            nc.sync.dma_start(out=t[:, 1], in_=w_a[h].rearrange("(r p) o -> p r o", r=4))
+            nc.sync.dma_start(out=t[:, 0], in_=w_in[h].rearrange("(p r) o -> p r o", r=4))
+            nc.sync.dma_start(out=t[:, 1], in_=w_a[h].rearrange("(p r) o -> p r o", r=4))
             wraw[h] = t
 
         LOADS = dict(A=load_ga, G=load_g, Y=load_gx, X=load_x, S=load_s, W=load_w)
@@ -336,13 +336,13 @@ def tile_rglru_v_kernel(tc, x, state, w_in, b_in, w_a, b_a, a_param, gate_x, gat
 
         def v_w(h, a, q):
             if q == 0:
-                wf[h, a] = st([P, 4, P, 4], BF16, "Fq", 2)
-            nc.vector.tensor_copy(out=wf[h, a][:].bitcast(F32)[:, 2 * q:2 * q + 2],
-                                  in_=wb[h, a, q][:].rearrange("p r u n -> p r n u"))
+                wf[h, a] = st([P, P, 4, 4], BF16, "Fq", 2)
+            nc.vector.tensor_copy(out=wf[h, a][:].bitcast(F32)[:, :, 2 * q:2 * q + 2, :],
+                                  in_=wb[h, a, q][:].rearrange("p r u n -> p n r u"))
 
         def v_qw(h, a):
             wc[h, a] = codes("w", 4)
-            v_quant(wf[h, a][:].rearrange("p r n t -> p (r n t)"), wc[h, a], E4)
+            v_quant(wf[h, a][:].rearrange("p n r t -> p (n r t)"), wc[h, a], E4)
 
         xi, xc = {}, {}
 
@@ -425,7 +425,7 @@ def tile_rglru_v_kernel(tc, x, state, w_in, b_in, w_a, b_a, a_param, gate_x, gat
             v_qw(h, 1)
             v_qw(h, 0)
 
-        G1 = 8
+        G1 = 6
         if W0AT >= 0:
             at(W0AT, "pe", w_evac, 0)
             at(W0AT, "end", w_quant, 0)

from contextlib import ExitStack

import concourse.mybir as mybir
from concourse.masks import make_identity

F32 = mybir.dt.float32
BF16 = mybir.dt.bfloat16
U32 = mybir.dt.uint32
U8 = mybir.dt.uint8
E4 = mybir.dt.float8_e4m3fn_x4
E5 = mybir.dt.float8_e5m2_x4
ACT = mybir.ActivationFunctionType
ALU = mybir.AluOpType

T, W, H, HD = 1024, 1024, 2, 512
P = 128
NG = 2
NM = NG * H
NC = 4 * NM

ORDER = "A0 A1 W0 G0 Y0 X0 S0 W1 A2 A3 G1 Y1 X1 S1"
W0AT = -1
W1AT = 0
W1SL = "p1"
EIT = 0
EITSL = "p1"
X0AT = 0
OB = 4
VADD = 0
VX = ()
FLAST = False
HB = 2
HEADWARM = 0
NW = lambda k, i: 3 if k == "ST" else 0
FLOPS = 2 * T * HD * 2 * HD * H + 2 * HD * HD * T * H


def tile_rglru_v_kernel(tc, x, state, w_in, b_in, w_a, b_a, a_param, gate_x, gate_a, grad_out, out_0, out_1):
    nc = tc.nc

    def tok(ap):
        return ap.rearrange("(g p j) w -> g p j w", g=NG, j=4)

    xv, sv, gv, gxv, gav, ov = tok(x), tok(state), tok(grad_out), tok(gate_x), tok(gate_a), tok(out_0)

    with ExitStack() as ctx:
        sb = ctx.enter_context(tc.tile_pool(name="sb", bufs=1))
        ps = ctx.enter_context(tc.psum_pool(name="ps", bufs=1))
        ctx.enter_context(tc.manual_schedule())

        def st(shape, dt, tag, bufs):
            return sb.tile(shape, dt, name=tag, tag=tag, bufs=bufs, align_bytes=64)

        def bank(shape, tag, bufs):
            return ps.tile(shape, F32, name=tag, tag=tag, bufs=bufs)

        rows = st([P, P], F32, "rows", 1)
        nc.vector.memset(rows[:], 0.0)
        raw = st([P, P], BF16, "apar", 1)
        nc.sync.dma_start(out=raw[:8, :], in_=a_param.rearrange("(k p) -> k p", p=P))
        ident = st([P, P], F32, "ident", 1)
        make_identity(nc, ident[:])
        one = st([P, 1], F32, "one", 1)
        negone = st([P, 1], F32, "negone", 1)
        neghalf = st([P, 1], F32, "neghalf", 1)
        nc.vector.memset(one[:], 1.0)
        nc.vector.memset(negone[:], -1.0)
        nc.vector.memset(neghalf[:], -0.5)

        def pe_warm(b):
            nc.tensor.matmul(b[:, 0, :], lhsT=ident[:], rhs=ident[:], start=True, stop=True)

        ga, gx, gt, stt, xt = {}, {}, {}, {}, {}

        def load(dst, key, view, dt, tag, bufs, m):
            g, h = m // H, m % H
            t = st([P, 4, HD], dt, tag, bufs)
            nc.sync.dma_start(out=t[:], in_=view[g, :, :, h * HD:(h + 1) * HD])
            dst[key] = t

        def load_ga(m):
            load(ga, m, gav, F32, "ga", NM + 1, m)

        def load_gx(m):
            load(gx, m, gxv, F32, "gx", 2, m)

        def load_g(m):
            load(gt, m, gv, BF16, "g", 2, m)

        def load_s(m):
            load(stt, m, sv, BF16, "s", 2, m)

        def load_x(m):
            load(xt, m, xv, BF16, "x", 2, m)

        wraw = {}

        def load_w(h):
            t = st([P, 2, 4, HD], BF16, "e", 3)
            nc.sync.dma_start(out=t[:, 0], in_=w_in[h].rearrange("(p r) o -> p r o", r=4))
            nc.sync.dma_start(out=t[:, 1], in_=w_a[h].rearrange("(p r) o -> p r o", r=4))
            wraw[h] = t

        LOADS = dict(A=load_ga, G=load_g, Y=load_gx, X=load_x, S=load_s, W=load_w)
        for key in ORDER.split():
            LOADS[key[0]](int(key[1]))

        nc.vector.tensor_copy(out=rows[:8, :], in_=raw[:8, :])
        for n in range(HEADWARM):
            pe_warm(bank([P, 4, P], "DT", 1))
        apb = bank([P, P], "ST", 1)
        nc.tensor.transpose(apb[:], rows[:], ident[:])
        apf = apb[:, 0:8]
        nabs = st([P, 8], F32, "nabs", 1)
        relu = st([P, 8], F32, "relu", 1)
        u8 = st([P, 8], F32, "u8", 1)
        l8 = st([P, 8], F32, "l8", 1)
        sp = st([P, 8], F32, "sp", 1)
        c8 = st([P, 8], F32, "c8", 1)
        c16 = st([P, 8], F32, "c16", 1)
        nc.vector.tensor_scalar(out=relu[:], in0=apf, scalar1=0.0, scalar2=None, op0=ALU.max)
        nc.vector.scalar_tensor_tensor(out=nabs[:], in0=relu[:], scalar=-2.0, in1=apf, op0=ALU.mult, op1=ALU.add)
        nc.scalar.activation(out=u8[:], in_=nabs[:], func=ACT.Exp)
        nc.scalar.activation(out=l8[:], in_=u8[:], func=ACT.Ln, bias=one[:])
        nc.vector.tensor_tensor(out=sp[:], in0=l8[:], in1=relu[:], op=ALU.add)
        nc.vector.tensor_scalar(out=c16[:], in0=sp[:], scalar1=16.0, scalar2=None, op0=ALU.mult)
        nc.vector.tensor_scalar(out=c8[:], in0=sp[:], scalar1=8.0, scalar2=None, op0=ALU.mult)

        def mh(i):
            return i // 4, (i // 4) % H, i % 4

        gab, ea, qp, sc = {}, {}, {}, {}

        def pe_ga(i):
            m, h, t = mh(i)
            b = bank([P, 4, P], "X", 4)
            for rep in range(NW("GA", i)):
                pe_warm(b)
            for j in range(4):
                nc.tensor.transpose(b[:, j, :], ga[m][:, j, t * P:(t + 1) * P], ident[:])
            gab[i] = b

        def s_e(i):
            m, h, t = mh(i)
            ea[i] = st([P, HD], F32, "EA", NC)
            nc.scalar.activation(out=ea[i][:], in_=gab[i][:].rearrange("p j n -> p (j n)"), func=ACT.Exp,
                                 scale=c16[:, 4 * h + t:4 * h + t + 1])

        def s_q(i):
            qp[i] = st([P, HD], F32, "qp", 4)
            nc.scalar.activation(out=qp[i][:], in_=ea[i][:], func=ACT.Abs_reciprocal_sqrt, bias=negone[:])

        def s_a(i):
            nc.scalar.activation(out=ea[i][:], in_=ea[i][:], func=ACT.Abs_reciprocal_sqrt)

        def s_p(i):
            nc.scalar.activation(out=qp[i][:], in_=qp[i][:], func=ACT.Square)

        def s_s(i):
            sc[i] = st([P, 4, P], F32, "S", 2)
            nc.scalar.activation(out=sc[i][:].rearrange("p j n -> p (j n)"), in_=qp[i][:],
                                 func=ACT.Abs_reciprocal_sqrt, bias=one[:])

        sq = {}

        def s_sq(m):
            sq[m] = st([P, HD, 4], F32, "ga", NM + 1)
            nc.scalar.activation(out=sq[m][:], in_=ga[m][:].rearrange("p j w -> p w j"), func=ACT.Square, bias=neghalf[:])

        hh, tt = {}, {}

        def g_h(i):
            m, h, t = mh(i)
            hh[i] = st([P, 4 * P + 8], F32, "h", HB)
            if HB == 2:
                nc.gpsimd.memset(hh[i][:, 4 * P:4 * P + 1], -1.0)
            nc.gpsimd.tensor_tensor(out=hh[i][:, :4 * P].rearrange("p (j f) -> p j f", j=4), in0=gt[m][:, :, t * P:(t + 1) * P], in1=gx[m][:, :, t * P:(t + 1) * P], op=ALU.mult)

        def g_t(i):
            m, h, t = mh(i)
            tt[i] = st([P, 4, P], F32, "t", 2)
            nc.gpsimd.tensor_tensor(out=tt[i][:], in0=gt[m][:, :, t * P:(t + 1) * P], in1=stt[m][:, :, t * P:(t + 1) * P], op=ALU.mult)

        stb, tfb, ffb, dtb = {}, {}, {}, {}
        ee, ff, dpa, nd = {}, {}, {}, {}
        d1, d2 = {}, {}

        def pe_st(i):
            b = bank([P, 4, P], "ST", 1)
            for rep in range(NW("ST", i)):
                pe_warm(b)
            for j in range(4):
                nc.tensor.transpose(b[:, j, :], sc[i][:, j, :], ident[:])
            stb[i] = b

        def v_e(i):
            m, h, t = mh(i)
            if t == 0:
                ee[m] = st([P, 4, HD], F32, "e", 3)
            nc.vector.tensor_tensor(out=ee[m][:, :, t * P:(t + 1) * P], in0=stb[i][:], in1=hh[i][:, :4 * P].rearrange("p (j f) -> p j f", j=4), op=ALU.mult)

        def v_f(i):
            m, h, t = mh(i)
            if t == 0:
                ff[m] = st([P, 4, HD], F32, "f", 2)
            cols = slice(t * P, (t + 1) * P)
            nc.vector.scalar_tensor_tensor(out=ff[m][:, :, cols], in0=ee[m][:, :, cols], scalar=hh[i][:, 4 * P:4 * P + 1] if HB == 2 else -1.0, in1=xt[m][:, :, cols], op0=ALU.mult, op1=ALU.mult)

        def pe_ff(i):
            m, h, t = mh(i)
            b = bank([P, 4, P], "FF", 1)
            for rep in range(NW("FF", i)):
                pe_warm(b)
            for j in range(4):
                nc.tensor.transpose(b[:, j, :], ff[m][:, j, t * P:(t + 1) * P], ident[:])
            ffb[i] = b

        def pe_tf(i):
            b = bank([P, 4, P], "TF", 1)
            for rep in range(NW("TF", i)):
                pe_warm(b)
            for j in range(4):
                nc.tensor.transpose(b[:, j, :], tt[i][:, j, :], ident[:])
            tfb[i] = b

        def v_d1(i):
            m, h, t = mh(i)
            d1[i] = st([P, 4, P], F32, "d1", 1)
            nc.vector.scalar_tensor_tensor(out=d1[i][:].rearrange("p j n -> p (j n)"),
                                           in0=tfb[i][:].rearrange("p j n -> p (j n)"),
                                           scalar=c8[:, 4 * h + t:4 * h + t + 1],
                                           in1=ea[i][:], op0=ALU.mult, op1=ALU.mult)

        def v_d2(i):
            m, h, t = mh(i)
            d2[i] = st([P, 4, P], F32, "d2", 1)
            nc.vector.scalar_tensor_tensor(out=d2[i][:].rearrange("p j n -> p (j n)"),
                                           in0=ffb[i][:].rearrange("p j n -> p (j n)"),
                                           scalar=c8[:, 4 * h + t:4 * h + t + 1],
                                           in1=qp[i][:], op0=ALU.mult, op1=ALU.mult)

        def v_add(i):
            nc.vector.tensor_tensor(out=d1[i][:], in0=d1[i][:], in1=d2[i][:], op=ALU.add)

        def pe_dt(i):
            b = bank([P, 4, P], "DT", 1)
            for j in range(4):
                if i < VADD:
                    nc.tensor.transpose(b[:, j, :], d1[i][:, j, :], ident[:])
                    continue
                nc.tensor.matmul(b[:, j, :], lhsT=d1[i][:, j, :], rhs=ident[:], start=True, stop=False, is_transpose=True)
                nc.tensor.matmul(b[:, j, :], lhsT=d2[i][:, j, :], rhs=ident[:], start=False, stop=True, is_transpose=True)
            dtb[i] = b

        def v_dpa(i):
            m, h, t = mh(i)
            if t == 0:
                dpa[m] = st([P, HD, 4], BF16, "dpaT", 1)
            nc.vector.scalar_tensor_tensor(out=dpa[m][:, t * P:(t + 1) * P],
                                           in0=sq[m][:, t * P:(t + 1) * P], scalar=0.25,
                                           in1=dtb[i][:].rearrange("p j f -> p f j"),
                                           op0=ALU.subtract, op1=ALU.mult)

        def v_ndp(m, q):
            if q == 0:
                nd[m] = st([P, 4, HD], BF16, "ndp", 1)
            js = slice(2 * q, 2 * q + 2)
            nc.vector.scalar_tensor_tensor(out=nd[m][:, js], in0=gx[m][:, js], scalar=1.0, in1=ff[m][:, js],
                                           op0=ALU.subtract, op1=ALU.mult)

        dib, dab, dif, daf = {}, {}, {}, {}
        dinc, dafc, dtc = {}, {}, {}

        def codes(tag, bufs):
            return st([P, HD], U32, tag + "_c", bufs), st([P, HD], U8, tag + "_s", bufs)

        def pe_di(m, q):
            b = bank([P, 2, 2, P], "X", 4)
            words = nd[m][:].bitcast(F32)
            for r in range(2):
                for u in range(2):
                    nc.tensor.transpose(b[:, r, u, :], words[:, 2 * q + r, u::2], ident[:])
            dib[m, q] = b

        def s_di(m, q):
            if q == 0:
                dif[m] = st([P, 4, P, 4], BF16, "Fq", 2)
            nc.scalar.copy(out=dif[m][:].bitcast(F32)[:, 2 * q:2 * q + 2], in_=dib[m, q][:].rearrange("p r u n -> p r n u"))

        def pe_da(m, v):
            b = bank([P, 4, P], "X", 4)
            words = dpa[m][:].bitcast(F32)
            for t in range(4):
                nc.tensor.transpose(b[:, t, :], words[:, t::4, v], ident[:])
            dab[m, v] = b

        def s_da(m, v):
            if v == 0:
                daf[m] = st([P, 4, P, 4], BF16, "Fq", 2)
            nc.scalar.copy(out=daf[m][:, 2 * v:2 * v + 2],
                           in_=dab[m, v][:].bitcast(BF16).rearrange("p t (n e) -> p e n t", e=2))

        def v_da(m, v):
            if v == 0:
                daf[m] = st([P, 4, P, 4], BF16, "Fq", 2)
            nc.vector.tensor_copy(out=daf[m][:, 2 * v:2 * v + 2],
                                  in_=dab[m, v][:].bitcast(BF16).rearrange("p t (n e) -> p e n t", e=2))

        def v_quant(src, pair, fmt):
            c, s = pair
            nc.vector.quantize_mx(out=c[:].bitcast(fmt), scales=s[:], in_=src)

        def v_qdi(m):
            dinc[m] = codes("di", 1)
            v_quant(dif[m][:].rearrange("p j n t -> p (j n t)"), dinc[m], E5)

        def v_qda(m):
            dafc[m] = codes("da", 1)
            v_quant(daf[m][:].rearrange("p j n t -> p (j n t)"), dafc[m], E5)

        def v_qdt(m):
            dtc[m] = codes("dt", 4)
            v_quant(dpa[m][:].rearrange("p w j -> p (w j)"), dtc[m], E5)

        wb, wf, wc = {}, {}, {}

        def pe_w(h, a, q):
            b = bank([P, 2, 2, P], "X", 4)
            if NW("W", 4 * h + 2 * (1 - a) + q):
                pe_warm(b[:, 0])
            words = wraw[h][:].bitcast(F32)
            for r in range(2):
                for u in range(2):
                    nc.tensor.transpose(b[:, r, u, :], words[:, a, 2 * q + r, u::2], ident[:])
            wb[h, a, q] = b

        def v_w(h, a, q):
            if q == 0:
                wf[h, a] = st([P, P, 4, 4], BF16, "Fq", 2)
            nc.vector.tensor_copy(out=wf[h, a][:].bitcast(F32)[:, :, 2 * q:2 * q + 2, :],
                                  in_=wb[h, a, q][:].rearrange("p r u n -> p n r u"))

        def v_qw(h, a):
            wc[h, a] = codes("w", 4)
            v_quant(wf[h, a][:].rearrange("p n r t -> p (n r t)"), wc[h, a], E4)

        xi, xc = {}, {}

        def x_int(m, copy):
            xi[m] = st([P, HD, 4], BF16, "ndp", 1)
            copy(out=xi[m][:].rearrange("p (c i) t -> p c t i", i=4), in_=xt[m][:].rearrange("p t (c i) -> p c t i", i=4))

        def v_xint(m):
            x_int(m, nc.vector.tensor_copy)

        def s_xint(m):
            x_int(m, nc.scalar.copy)

        def v_qx(m):
            xc[m] = codes("x", 4)
            v_quant(xi[m][:].rearrange("p w j -> p (w j)"), xc[m], E4)

        def v_qda_half(m, v):
            if v == 0:
                dafc[m] = codes("da", 1)
            c, s = dafc[m]
            cols = slice(256 * v, 256 * (v + 1))
            nc.vector.quantize_mx(out=c[:, cols].bitcast(E5), scales=s[:, cols],
                                  in_=daf[m][:, 2 * v:2 * v + 2].rearrange("p j n t -> p (j n t)"))

        mmb, dwb = {}, {}

        def pe_mm_part(m, j, n):
            h = m % H
            if n == 0:
                mmb[m, j] = bank([P, HD], "X", 4)
            cols = slice(j * P, (j + 1) * P)
            d = (dinc, dafc)[n][m]
            nc.tensor.matmul_mx(out=mmb[m, j][:], lhsT=d[0][:, cols].bitcast(E5), lhsT_scale=d[1][:, cols],
                                rhs=wc[h, n][0][:].bitcast(E4), rhs_scale=wc[h, n][1][:],
                                start=(n == 0), stop=(n == 1))

        def pe_mm(m, j):
            pe_mm_part(m, j, 0)
            pe_mm_part(m, j, 1)

        def v_fin(m, j):
            g, h = m // H, m % H
            o = st([P, HD], F32, "o", OB)
            nc.vector.tensor_tensor(out=o[:], in0=mmb[m, j][:], in1=ee[m][:, j, :], op=ALU.add)
            nc.sync.dma_start(out=ov[g, :, j, h * HD:(h + 1) * HD], in_=o[:])

        def pe_dw(h, c, tag="X", bufs=4):
            b = bank([P, HD], tag, bufs)
            cols = slice(c * P, (c + 1) * P)
            for g in range(NG):
                m = g * H + h
                nc.tensor.matmul_mx(out=b[:], lhsT=xc[m][0][:, cols].bitcast(E4), lhsT_scale=xc[m][1][:, cols],
                                    rhs=dtc[m][0][:].bitcast(E5), rhs_scale=dtc[m][1][:],
                                    start=(g == 0), stop=(g == NG - 1))
            dwb[h, c] = b

        def s_dw(h, c, tag, bufs):
            o = st([P, HD], F32, tag, bufs)
            nc.scalar.copy(out=o[:], in_=dwb[h, c][:])
            nc.sync.dma_start(out=out_1[h, c * P:(c + 1) * P, :], in_=o[:])

        plan = {}
        ADDS = []

        def at(i, slot, fn, *args):
            plan.setdefault((i, slot), []).append((fn, args))

        def run(i, slot):
            for fn, args in plan.get((i, slot), ()):
                fn(*args)

        def w_evac(h):
            for a in (1, 0):
                for q in range(2):
                    pe_w(h, a, q)
                    v_w(h, a, q)

        def w_quant(h):
            v_qw(h, 1)
            v_qw(h, 0)

        G1 = 6
        if W0AT >= 0:
            at(W0AT, "pe", w_evac, 0)
            at(W0AT, "end", w_quant, 0)
        at(W1AT, W1SL, w_evac, 1)
        at(W1AT, "end", w_quant, 1)
        for k in range(G1, NC):
            at(EIT, EITSL, pe_ga, k)
            at(EIT, EITSL, s_e, k)
        for m in range(NM):
            if m == 0:
                at(X0AT, "end", v_xint, m)
                at(X0AT + 1, "end", v_qx, m)
            else:
                if m in VX:
                    at(4 * m + 2, "end", v_xint, m)
                else:
                    at(4 * m + 2, "x", s_xint, m)
                at(4 * m + 3, "end", v_qx, m)
            if m:
                at(4 * m, "s1", s_sq, m)
        LAST = NM - 1
        for m in range(NM):
            b = 4 * m + 4
            if m < LAST:
                at(b, "end", v_ndp, m, 0)
                at(b, "end", pe_di, m, 0)
                at(b + 1, "s0", s_di, m, 0)
                for v in range(2):
                    at(b + 1, "pe", pe_da, m, v)
                    at(b + 1, "pe", s_da, m, v)
                at(b + 1, "end0", v_ndp, m, 1)
                at(b + 1, "end0", pe_di, m, 1)
                at(b + 1, "end0", v_qdt, m)
                at(b + 2, "s0", s_di, m, 1)
                at(b + 2, "end", v_qda, m)
                at(b + 2, "end", v_qdi, m)
                for j in range(4):
                    at(b + 2 + j, "end", pe_mm, m, j)
                    at(b + 3 + j, "fin", v_fin, m, j)
            else:
                at(b, "p1", v_ndp, m, 0)
                at(b, "p1", pe_di, m, 0)
                at(b, "p1", s_di, m, 0)
                at(b, "end", v_ndp, m, 1)
                at(b, "end", pe_di, m, 1)
                at(b, "end", s_di, m, 1)
                at(b + 1, "pe", pe_da, m, 0)
                at(b + 1, "pe", s_da, m, 0)
                at(b + 1, "pe", pe_da, m, 1)
                at(b + 1, "pe", v_qdt, m)
                at(b + 1, "pe", v_qdi, m)
                at(b + 1, "pe", v_da, m, 1)
                tags = ("ST", "FF", "TF", "DT")
                at(b + 2, "fin", pe_mm_part, m, 0, 0)
                at(b + 2, "fin", pe_mm_part, m, 1, 0)
                for c in range(4):
                    at(b + 2, "fin", pe_dw, 1, c, tags[c], 1)
                at(b + 2, "fin", v_qda_half, m, 0)
                at(b + 2, "fin", pe_mm_part, m, 0, 1)
                at(b + 2, "fin", pe_mm_part, m, 1, 1)
                at(b + 2, "fin", pe_mm_part, m, 2, 0)
                at(b + 2, "fin", pe_mm_part, m, 3, 0)
                at(b + 2, "fin", v_qda_half, m, 1)
                at(b + 2, "fin", pe_mm_part, m, 2, 1)
                at(b + 2, "fin", pe_mm_part, m, 3, 1)
                for c in range(4):
                    at(b + 2, "fin", s_dw, 1, c, ("S", "t")[c % 2], 2)
                for j in range(4):
                    at(b + 2, "fin2", v_fin, m, j)
            if m == 2:
                for c in range(4):
                    at(b + 2 + c // 2, "end", pe_dw, 0, c)
                    at(b + 3 + c // 2, "s0", s_dw, 0, c, "o", OB)
            if m + 2 < NM:
                at(b, "s0", load_g, m + 2)
                at(b, "s0", load_s, m + 2)
                at(b, "s0", load_x, m + 2)
                at(b + 1, "end0", load_gx, m + 2)

        for k in range(G1):
            pe_ga(k)
            s_e(k)
        if W0AT < 0:
            w_evac(0)
            w_quant(0)
        g_h(0)
        g_t(0)
        if HB == 2:
            g_h(1)
            g_t(1)
        s_q(0)
        s_q(1)
        s_p(0)
        s_a(0)
        s_s(0)
        pe_st(0)
        s_p(1)
        s_a(1)
        s_s(1)
        for i in range(NC + 8):
            run(i, "s0")
            if i + 2 < NC:
                s_q(i + 2)
                s_a(i + 2)
                s_p(i + 2)
                run(i, "s1")
                s_s(i + 2)
                if i == 0:
                    s_sq(0)
            run(i, "x")
            if i < NC:
                v_e(i)
            if i + 1 < NC:
                if HB == 1:
                    g_h(i + 1)
                    g_t(i + 1)
                pe_st(i + 1)
            if 1 <= i <= NC:
                v_d1(i - 1)
                v_d2(i - 1)
                if i - 1 < VADD:
                    ADDS.append(i - 1)
            run(i, "p1")
            if i < NC:
                pe_tf(i)
            if 2 <= i <= NC + 1:
                v_dpa(i - 2)
            if ADDS:
                v_add(ADDS.pop())
            if 1 <= i <= NC:
                pe_dt(i - 1)
            run(i, "fin")
            run(i, "fin2")
            while ADDS:
                v_add(ADDS.pop())
            run(i, "pe")
            if i < NC:
                if not FLAST:
                    v_f(i)
                    pe_ff(i)
            run(i, "end0")
            run(i, "end")
            if i < NC and FLAST:
                v_f(i)
                pe_ff(i)
            if HB == 2 and i + 2 < NC:
                g_h(i + 2)
                g_t(i + 2)
